import numpy as np
import ml_dtypes


def mxq(x, axis, fmt="e4m3"):
    dtype, down = {"e4m3": (ml_dtypes.float8_e4m3fn, 7), "e5m2": (ml_dtypes.float8_e5m2, 14)}[fmt]
    v = np.moveaxis(np.asarray(x, np.float32).astype(ml_dtypes.bfloat16).astype(np.float64), axis, -1)
    blocks = v.reshape(v.shape[:-1] + (-1, 32))
    amax = np.abs(blocks).max(-1, keepdims=True)
    byte = np.maximum(np.where(amax > 0, np.frexp(amax)[1] - 1 + 127, 0) - down, 1)
    scale = np.exp2(byte - 127.0)
    codes = (blocks / scale).astype(np.float32).astype(dtype).astype(np.float64)
    return np.moveaxis((codes * scale).reshape(v.shape), -1, axis)


WIDE = False


def mx_kscale(k):
    if not WIDE:
        return np.ones(k)
    levels = np.array([10, -10, 5, -5, 0])
    a = np.random.permutation(np.resize(levels, k // 512 * 4)).reshape(k // 512, 4)
    idx = np.arange(k)
    return np.exp2(a[idx // 512, idx % 128 // 32])


BF16 = ml_dtypes.bfloat16


def bf(x):
    return np.asarray(x, np.float32).astype(BF16)


def f64(x):
    return np.asarray(x).astype(np.float64)


B, N, SIZE, CH = 128, 16, 1024, 256


def sigmoid(v):
    return 1.0 / (1.0 + np.exp(-v))


def setup_inputs():
    s = mx_kscale(SIZE)
    d = {"z0": bf(np.random.standard_normal((B, SIZE)) * s),
         "h_tilde": bf(np.random.standard_normal((B, CH)) * np.sqrt(N)),
         "fc_sum": bf(np.random.standard_normal((B, CH)) * 1.2)}
    for g in ("i", "o", "u"):
        d["W_" + g] = bf(np.random.standard_normal((CH, SIZE)) / np.sqrt(SIZE) / s)
        d["U_" + g] = bf(np.random.standard_normal((CH, CH)) / np.sqrt(CH * N))
        d["b_" + g] = bf(np.random.standard_normal(CH) * 0.5)
    return d


def reference(z0, h_tilde, fc_sum, W_i, U_i, b_i, W_o, U_o, b_o, W_u, U_u, b_u):
    zq = mxq(f64(z0), 1, "e4m3")
    ht = f64(h_tilde)
    i_j = sigmoid((zq @ mxq(f64(W_i), 1, "e4m3").T) + ht @ f64(U_i).T + f64(b_i))
    o_j = sigmoid((zq @ mxq(f64(W_o), 1, "e4m3").T) + ht @ f64(U_o).T + f64(b_o))
    u_j = np.tanh((zq @ mxq(f64(W_u), 1, "e4m3").T) + ht @ f64(U_u).T + f64(b_u))
    c_j = i_j * u_j + f64(fc_sum)
    h_j = o_j * np.tanh(c_j)
    return np.concatenate([h_j, c_j], axis=-1)

@@ -1,0 +1,178 @@
+from contextlib import ExitStack
+
+import concourse.mybir as mybir
+from concourse.masks import make_identity
+
+F32 = mybir.dt.float32
+BF16 = mybir.dt.bfloat16
+U32 = mybir.dt.uint32
+U8 = mybir.dt.uint8
+FP8X4 = mybir.dt.float8_e4m3fn_x4
+ACT = mybir.ActivationFunctionType
+ALU = mybir.AluOpType
+
+P = 128
+SIZE = 1024
+CH = 256
+GATES = 3
+ROW_BLOCKS = CH // P
+PASSES = SIZE // (4 * P)
+HALVES = 2
+WORDS = PASSES * P
+BANK_SLOTS = 4
+
+FLOPS = 2 * P * GATES * CH * (SIZE + CH)
+
+
+def transpose_pairs(nc, bank, slot, words, ident):
+    nc.tensor.transpose(out=bank[:, slot, :], in_=words, identity=ident[:])
+
+
+def quantise_rows(nc, banks, stage, rows, ident, codes, scales):
+    words = rows[:].bitcast(F32)
+    bank = banks.tile([P, BANK_SLOTS, P], F32, tag="bank", name="bank")
+    for slot in range(PASSES * HALVES):
+        transpose_pairs(nc, bank, slot, words[:, slot * P : (slot + 1) * P], ident)
+    grouped = stage.tile([P, SIZE], BF16, align_bytes=64, name="grouped")
+    nc.scalar.copy(
+        out=grouped[:].bitcast(F32).rearrange("p (g r u) -> p g r u", g=PASSES, u=HALVES),
+        in_=bank[:].rearrange("p (g u) r -> p g r u", u=HALVES),
+    )
+    nc.vector.quantize_mx(out=codes.bitcast(FP8X4), scales=scales, in_=grouped[:])
+
+
+def tile_treelstm_pb_s_kernel(
+    tc, z0, h_tilde, fc_sum, W_i, U_i, b_i, W_o, U_o, b_o, W_u, U_u, b_u, out
+):
+    nc = tc.nc
+    gate_w = (W_i, W_u, W_o)
+    gate_u = (U_i, U_u, U_o)
+    gate_b = (b_i, b_u, b_o)
+
+    with ExitStack() as pools:
+        keep = pools.enter_context(tc.tile_pool(name="keep", bufs=1))
+        w_pool = pools.enter_context(tc.tile_pool(name="w_rows", bufs=GATES * ROW_BLOCKS))
+        stage = pools.enter_context(tc.tile_pool(name="stage", bufs=4))
+        banks = pools.enter_context(tc.psum_pool(name="banks", bufs=5))
+        sums = pools.enter_context(tc.psum_pool(name="sums", bufs=GATES))
+
+        ident = keep.tile([P, P], F32, name="ident")
+        make_identity(nc, ident[:])
+        warm = keep.tile([P, 1], F32, name="warm")
+        nc.vector.memset(warm[:], 0.0)
+        nc.scalar.activation(out=warm[:], in_=warm[:], func=ACT.Sigmoid)
+
+        bias_rows = keep.tile([P, CH], BF16, name="bias_rows")
+        nc.vector.memset(bias_rows[:], 0.0)
+        for g in range(GATES):
+            nc.sync.dma_start(
+                out=bias_rows[g : g + 1, :], in_=gate_b[g].rearrange("(o c) -> o c", o=1)
+            )
+        z_rows = keep.tile([P, SIZE], BF16, name="z_rows")
+        nc.sync.dma_start(out=z_rows[:], in_=z0[:, :])
+        h_rows = keep.tile([P, CH], BF16, name="h_rows")
+        nc.sync.dma_start(out=h_rows[:], in_=h_tilde[:, :])
+        u_rows = []
+        for g in range(GATES):
+            rows = keep.tile([P, ROW_BLOCKS * CH], BF16, name="u_rows_%d" % g)
+            nc.sync.dma_start(
+                out=rows[:].rearrange("p (b k) -> p b k", b=ROW_BLOCKS),
+                in_=gate_u[g].rearrange("(b p) k -> p b k", p=P),
+            )
+            u_rows.append(rows)
+        w_rows = []
+        for g in range(GATES):
+            for b in range(ROW_BLOCKS):
+                rows = w_pool.tile([P, SIZE], BF16, name="w_rows")
+                nc.sync.dma_start(out=rows[:], in_=gate_w[g][b * P : (b + 1) * P, :])
+                w_rows.append(rows)
+        fc = keep.tile([P, CH], BF16, name="fc")
+        nc.sync.dma_start(out=fc[:], in_=fc_sum[:, :])
+
+        bank = banks.tile([P, BANK_SLOTS, P], F32, tag="bank", name="bank")
+        transpose_pairs(nc, bank, 0, bias_rows[:].bitcast(F32), ident)
+        bias_cols = keep.tile([P, GATES], F32, name="bias_cols")
+        nc.vector.tensor_copy(out=bias_cols[:], in_=bank[:, 0, 0:GATES])
+        bank = banks.tile([P, BANK_SLOTS, P], F32, tag="bank", name="bank")
+        for g in range(GATES):
+            transpose_pairs(nc, bank, g, bias_cols[:, g : g + 1].to_broadcast([P, P]), ident)
+        bias_all = keep.tile([P, GATES * CH], BF16, name="bias_all")
+        nc.vector.tensor_copy(
+            out=bias_all[:].bitcast(F32).rearrange("p (g w) -> p g w", g=GATES),
+            in_=bank[:, 0:GATES, :],
+        )
+
+        z_codes = keep.tile([P, WORDS], U32, align_bytes=64, name="z_codes")
+        z_scales = keep.tile([P, WORDS], U8, align_bytes=64, name="z_scales")
+        quantise_rows(nc, banks, stage, z_rows, ident, z_codes[:], z_scales[:])
+
+        blocks = [u_rows[g][:].bitcast(F32)[:, b * P : (b + 1) * P]
+                  for g in range(GATES) for b in range(ROW_BLOCKS)]
+        blocks.append(h_rows[:].bitcast(F32))
+        pairs_t = keep.tile([P, len(blocks), P], F32, name="pairs_t")
+        for first in range(0, len(blocks), BANK_SLOTS):
+            group = blocks[first : first + BANK_SLOTS]
+            bank = banks.tile([P, BANK_SLOTS, P], F32, tag="bank", name="bank")
+            for slot in range(len(group)):
+                transpose_pairs(nc, bank, slot, group[slot], ident)
+            nc.vector.tensor_copy(
+                out=pairs_t[:, first : first + len(group), :], in_=bank[:, 0 : len(group), :]
+            )
+        by_parity = pairs_t[:].rearrange("p s r -> p (s r)").bitcast(BF16).rearrange(
+            "p (c e) -> p c e", e=2
+        )
+        h_first = GATES * CH
+        plain = []
+        for g in range(GATES):
+            plain_ps = sums.tile([P, CH], F32, tag="sums", name="plain_ps")
+            for e in range(2):
+                nc.tensor.matmul(
+                    out=plain_ps[:],
+                    lhsT=by_parity[:, h_first : h_first + P, e],
+                    rhs=by_parity[:, g * CH : (g + 1) * CH, e],
+                    start=(e == 0),
+                    stop=(e == 1),
+                )
+            plain_sb = keep.tile([P, CH], F32, name="plain_%d" % g)
+            nc.vector.tensor_tensor(
+                out=plain_sb[:], in0=plain_ps[:], in1=bias_all[:, g * CH : (g + 1) * CH], op=ALU.add
+            )
+            plain.append(plain_sb)
+
+        w_codes = keep.tile([P, len(w_rows), WORDS], U32, align_bytes=64, name="w_codes")
+        w_scales = keep.tile([P, len(w_rows), WORDS], U8, align_bytes=64, name="w_scales")
+        for j in range(len(w_rows)):
+            quantise_rows(nc, banks, stage, w_rows[j], ident, w_codes[:, j, :], w_scales[:, j, :])
+
+        acts = []
+        for g in range(GATES):
+            mx_ps = sums.tile([P, CH], F32, tag="sums", name="mx_ps")
+            for b in range(ROW_BLOCKS):
+                j = g * ROW_BLOCKS + b
+                for k_pass in range(PASSES):
+                    cols = slice(k_pass * P, (k_pass + 1) * P)
+                    nc.tensor.matmul_mx(
+                        out=mx_ps[:, b * P : (b + 1) * P],
+                        lhsT=z_codes[:, cols].bitcast(FP8X4),
+                        lhsT_scale=z_scales[:, cols],
+                        rhs=w_codes[:, j, cols].bitcast(FP8X4),
+                        rhs_scale=w_scales[:, j, cols],
+                        start=(k_pass == 0),
+                        stop=(k_pass == PASSES - 1),
+                    )
+            pre = keep.tile([P, CH], F32, name="pre_%d" % g)
+            nc.vector.tensor_tensor(out=pre[:], in0=mx_ps[:], in1=plain[g][:], op=ALU.add)
+            act = keep.tile([P, CH], F32, name="act_%d" % g)
+            nc.scalar.activation(out=act[:], in_=pre[:], func=(ACT.Tanh if g == 1 else ACT.Sigmoid))
+            acts.append(act)
+        gate_i, gate_u_act, gate_o = acts
+
+        c_sb = keep.tile([P, CH], F32, name="c_sb")
+        nc.vector.tensor_tensor(out=c_sb[:], in0=gate_i[:], in1=gate_u_act[:], op=ALU.mult)
+        nc.vector.tensor_tensor(out=c_sb[:], in0=c_sb[:], in1=fc[:], op=ALU.add)
+        nc.sync.dma_start(out=out[:, CH : 2 * CH], in_=c_sb[:])
+        tanh_c = keep.tile([P, CH], F32, name="tanh_c")
+        nc.scalar.activation(out=tanh_c[:], in_=c_sb[:], func=ACT.Tanh)
+        h_sb = keep.tile([P, CH], F32, name="h_sb")
+        nc.vector.tensor_tensor(out=h_sb[:], in0=gate_o[:], in1=tanh_c[:], op=ALU.mult)
+        nc.sync.dma_start(out=out[:, 0:CH], in_=h_sb[:])

@@ -20,6 +20,7 @@ PASSES = SIZE // (4 * P)
 HALVES = 2
 WORDS = PASSES * P
 BANK_SLOTS = 4
+WARM_UP = 12
 
 FLOPS = 2 * P * GATES * CH * (SIZE + CH)
 
@@ -28,11 +29,15 @@ def transpose_pairs(nc, bank, slot, words, ident):
     nc.tensor.transpose(out=bank[:, slot, :], in_=words, identity=ident[:])
 
 
-def quantise_rows(nc, banks, stage, rows, ident, codes, scales):
+def transpose_rows(nc, banks, rows, ident):
     words = rows[:].bitcast(F32)
     bank = banks.tile([P, BANK_SLOTS, P], F32, tag="bank", name="bank")
     for slot in range(PASSES * HALVES):
         transpose_pairs(nc, bank, slot, words[:, slot * P : (slot + 1) * P], ident)
+    return bank
+
+
+def pack_rows(nc, stage, bank, codes, scales):
     grouped = stage.tile([P, SIZE], BF16, align_bytes=64, name="grouped")
     nc.scalar.copy(
         out=grouped[:].bitcast(F32).rearrange("p (g r u) -> p g r u", g=PASSES, u=HALVES),
@@ -45,28 +50,37 @@ def tile_treelstm_pb_s_kernel(
     tc, z0, h_tilde, fc_sum, W_i, U_i, b_i, W_o, U_o, b_o, W_u, U_u, b_u, out
 ):
     nc = tc.nc
-    gate_w = (W_i, W_u, W_o)
-    gate_u = (U_i, U_u, U_o)
-    gate_b = (b_i, b_u, b_o)
+    w_dram = (W_i, W_u, W_o)
+    u_dram = (U_i, U_u, U_o)
+    b_dram = (b_i, b_u, b_o)
+    gate_func = (ACT.Sigmoid, ACT.Tanh, ACT.Sigmoid)
 
-    with ExitStack() as pools:
-        keep = pools.enter_context(tc.tile_pool(name="keep", bufs=1))
-        w_pool = pools.enter_context(tc.tile_pool(name="w_rows", bufs=GATES * ROW_BLOCKS))
-        stage = pools.enter_context(tc.tile_pool(name="stage", bufs=4))
-        banks = pools.enter_context(tc.psum_pool(name="banks", bufs=5))
-        sums = pools.enter_context(tc.psum_pool(name="sums", bufs=GATES))
+    with ExitStack() as ctx:
+        keep = ctx.enter_context(tc.tile_pool(name="keep", bufs=1))
+        w_pool = ctx.enter_context(tc.tile_pool(name="w_rows", bufs=GATES * ROW_BLOCKS))
+        stage = ctx.enter_context(tc.tile_pool(name="stage", bufs=4))
+        banks = ctx.enter_context(tc.psum_pool(name="banks", bufs=5))
+        sums = ctx.enter_context(tc.psum_pool(name="sums", bufs=GATES))
+        ctx.enter_context(tc.manual_schedule())
 
+        bias_rows = keep.tile([P, CH], BF16, name="bias_rows")
+        nc.vector.memset(bias_rows[:], 0.0)
         ident = keep.tile([P, P], F32, name="ident")
         make_identity(nc, ident[:])
+        idle_rows = keep.tile([P, SIZE], BF16, align_bytes=64, name="idle_rows")
+        idle_codes = keep.tile([P, WORDS], U32, align_bytes=64, name="idle_codes")
+        idle_scales = keep.tile([P, WORDS], U8, align_bytes=64, name="idle_scales")
+        nc.vector.memset(idle_rows[:], 0.0)
+        nc.vector.quantize_mx(
+            out=idle_codes[:].bitcast(FP8X4), scales=idle_scales[:], in_=idle_rows[:]
+        )
         warm = keep.tile([P, 1], F32, name="warm")
         nc.vector.memset(warm[:], 0.0)
         nc.scalar.activation(out=warm[:], in_=warm[:], func=ACT.Sigmoid)
 
-        bias_rows = keep.tile([P, CH], BF16, name="bias_rows")
-        nc.vector.memset(bias_rows[:], 0.0)
         for g in range(GATES):
             nc.sync.dma_start(
-                out=bias_rows[g : g + 1, :], in_=gate_b[g].rearrange("(o c) -> o c", o=1)
+                out=bias_rows[g : g + 1, :], in_=b_dram[g].rearrange("(o c) -> o c", o=1)
             )
         z_rows = keep.tile([P, SIZE], BF16, name="z_rows")
         nc.sync.dma_start(out=z_rows[:], in_=z0[:, :])
@@ -77,22 +91,37 @@ def tile_treelstm_pb_s_kernel(
             rows = keep.tile([P, ROW_BLOCKS * CH], BF16, name="u_rows_%d" % g)
             nc.sync.dma_start(
                 out=rows[:].rearrange("p (b k) -> p b k", b=ROW_BLOCKS),
-                in_=gate_u[g].rearrange("(b p) k -> p b k", p=P),
+                in_=u_dram[g].rearrange("(b p) k -> p b k", p=P),
             )
             u_rows.append(rows)
         w_rows = []
         for g in range(GATES):
             for b in range(ROW_BLOCKS):
                 rows = w_pool.tile([P, SIZE], BF16, name="w_rows")
-                nc.sync.dma_start(out=rows[:], in_=gate_w[g][b * P : (b + 1) * P, :])
+                nc.sync.dma_start(out=rows[:], in_=w_dram[g][b * P : (b + 1) * P, :])
                 w_rows.append(rows)
         fc = keep.tile([P, CH], BF16, name="fc")
         nc.sync.dma_start(out=fc[:], in_=fc_sum[:, :])
 
         bank = banks.tile([P, BANK_SLOTS, P], F32, tag="bank", name="bank")
+        for n in range(WARM_UP):
+            nc.tensor.matmul_mx(
+                out=bank[:].rearrange("p s r -> p (s r)")[:, 0:WORDS],
+                lhsT=idle_codes[:, 0:P].bitcast(FP8X4),
+                lhsT_scale=idle_scales[:, 0:P],
+                rhs=idle_codes[:].bitcast(FP8X4),
+                rhs_scale=idle_scales[:],
+                start=True,
+                stop=True,
+            )
+
+        bank = banks.tile([P, BANK_SLOTS, P], F32, tag="bank", name="bank")
         transpose_pairs(nc, bank, 0, bias_rows[:].bitcast(F32), ident)
         bias_cols = keep.tile([P, GATES], F32, name="bias_cols")
         nc.vector.tensor_copy(out=bias_cols[:], in_=bank[:, 0, 0:GATES])
+
+        z_bank = transpose_rows(nc, banks, z_rows, ident)
+
         bank = banks.tile([P, BANK_SLOTS, P], F32, tag="bank", name="bank")
         for g in range(GATES):
             transpose_pairs(nc, bank, g, bias_cols[:, g : g + 1].to_broadcast([P, P]), ident)
@@ -104,7 +133,7 @@ def tile_treelstm_pb_s_kernel(
 
         z_codes = keep.tile([P, WORDS], U32, align_bytes=64, name="z_codes")
         z_scales = keep.tile([P, WORDS], U8, align_bytes=64, name="z_scales")
-        quantise_rows(nc, banks, stage, z_rows, ident, z_codes[:], z_scales[:])
+        pack_rows(nc, stage, z_bank, z_codes[:], z_scales[:])
 
         blocks = [u_rows[g][:].bitcast(F32)[:, b * P : (b + 1) * P]
                   for g in range(GATES) for b in range(ROW_BLOCKS)]
@@ -122,10 +151,15 @@ def tile_treelstm_pb_s_kernel(
             "p (c e) -> p c e", e=2
         )
         h_first = GATES * CH
+
+        w_codes = keep.tile([P, len(w_rows), WORDS], U32, align_bytes=64, name="w_codes")
+        w_scales = keep.tile([P, len(w_rows), WORDS], U8, align_bytes=64, name="w_scales")
         plain = []
         for g in range(GATES):
             plain_ps = sums.tile([P, CH], F32, tag="sums", name="plain_ps")
-            for e in range(2):
+            for e in range(ROW_BLOCKS):
+                j = g * ROW_BLOCKS + e
+                w_bank = transpose_rows(nc, banks, w_rows[j], ident)
                 nc.tensor.matmul(
                     out=plain_ps[:],
                     lhsT=by_parity[:, h_first : h_first + P, e],
@@ -133,16 +167,16 @@ def tile_treelstm_pb_s_kernel(
                     start=(e == 0),
                     stop=(e == 1),
                 )
-            plain_sb = keep.tile([P, CH], F32, name="plain_%d" % g)
-            nc.vector.tensor_tensor(
-                out=plain_sb[:], in0=plain_ps[:], in1=bias_all[:, g * CH : (g + 1) * CH], op=ALU.add
-            )
-            plain.append(plain_sb)
-
-        w_codes = keep.tile([P, len(w_rows), WORDS], U32, align_bytes=64, name="w_codes")
-        w_scales = keep.tile([P, len(w_rows), WORDS], U8, align_bytes=64, name="w_scales")
-        for j in range(len(w_rows)):
-            quantise_rows(nc, banks, stage, w_rows[j], ident, w_codes[:, j, :], w_scales[:, j, :])
+                if e == 1:
+                    plain_sb = keep.tile([P, CH], F32, name="plain_%d" % g)
+                    nc.vector.tensor_tensor(
+                        out=plain_sb[:],
+                        in0=plain_ps[:],
+                        in1=bias_all[:, g * CH : (g + 1) * CH],
+                        op=ALU.add,
+                    )
+                    plain.append(plain_sb)
+                pack_rows(nc, stage, w_bank, w_codes[:, j, :], w_scales[:, j, :])
 
         acts = []
         for g in range(GATES):
@@ -163,16 +197,16 @@ def tile_treelstm_pb_s_kernel(
             pre = keep.tile([P, CH], F32, name="pre_%d" % g)
             nc.vector.tensor_tensor(out=pre[:], in0=mx_ps[:], in1=plain[g][:], op=ALU.add)
             act = keep.tile([P, CH], F32, name="act_%d" % g)
-            nc.scalar.activation(out=act[:], in_=pre[:], func=(ACT.Tanh if g == 1 else ACT.Sigmoid))
+            nc.scalar.activation(out=act[:], in_=pre[:], func=gate_func[g])
             acts.append(act)
-        gate_i, gate_u_act, gate_o = acts
+        act_i, act_u, act_o = acts
 
         c_sb = keep.tile([P, CH], F32, name="c_sb")
-        nc.vector.tensor_tensor(out=c_sb[:], in0=gate_i[:], in1=gate_u_act[:], op=ALU.mult)
+        nc.vector.tensor_tensor(out=c_sb[:], in0=act_i[:], in1=act_u[:], op=ALU.mult)
         nc.vector.tensor_tensor(out=c_sb[:], in0=c_sb[:], in1=fc[:], op=ALU.add)
         nc.sync.dma_start(out=out[:, CH : 2 * CH], in_=c_sb[:])
         tanh_c = keep.tile([P, CH], F32, name="tanh_c")
         nc.scalar.activation(out=tanh_c[:], in_=c_sb[:], func=ACT.Tanh)
         h_sb = keep.tile([P, CH], F32, name="h_sb")
-        nc.vector.tensor_tensor(out=h_sb[:], in0=gate_o[:], in1=tanh_c[:], op=ALU.mult)
+        nc.vector.tensor_tensor(out=h_sb[:], in0=act_o[:], in1=tanh_c[:], op=ALU.mult)
         nc.sync.dma_start(out=out[:, 0:CH], in_=h_sb[:])

@@ -20,20 +20,19 @@ PASSES = SIZE // (4 * P)
 HALVES = 2
 WORDS = PASSES * P
 BANK_SLOTS = 4
-WARM_UP = 12
 
 FLOPS = 2 * P * GATES * CH * (SIZE + CH)
 
 
-def transpose_pairs(nc, bank, slot, words, ident):
-    nc.tensor.transpose(out=bank[:, slot, :], in_=words, identity=ident[:])
+def word_blocks(rows):
+    words = rows.bitcast(F32)
+    return [words[:, s * P : (s + 1) * P] for s in range(words.shape[1] // P)]
 
 
-def transpose_rows(nc, banks, rows, ident):
-    words = rows[:].bitcast(F32)
+def transpose_words(nc, banks, blocks, ident):
     bank = banks.tile([P, BANK_SLOTS, P], F32, tag="bank", name="bank")
-    for slot in range(PASSES * HALVES):
-        transpose_pairs(nc, bank, slot, words[:, slot * P : (slot + 1) * P], ident)
+    for slot in range(len(blocks)):
+        nc.tensor.transpose(out=bank[:, slot, :], in_=blocks[slot], identity=ident[:])
     return bank
 
 
@@ -44,6 +43,10 @@ def pack_rows(nc, stage, bank, codes, scales):
         in_=bank[:].rearrange("p (g u) r -> p g r u", u=HALVES),
     )
     nc.vector.quantize_mx(out=codes.bitcast(FP8X4), scales=scales, in_=grouped[:])
+
+
+def by_parity(pairs, e):
+    return pairs[:].bitcast(BF16).rearrange("p (c e) -> p c e", e=2)[:, :, e]
 
 
 def tile_treelstm_pb_s_kernel(
@@ -57,7 +60,6 @@ def tile_treelstm_pb_s_kernel(
 
     with ExitStack() as ctx:
         keep = ctx.enter_context(tc.tile_pool(name="keep", bufs=1))
-        w_pool = ctx.enter_context(tc.tile_pool(name="w_rows", bufs=GATES * ROW_BLOCKS))
         stage = ctx.enter_context(tc.tile_pool(name="stage", bufs=4))
         banks = ctx.enter_context(tc.psum_pool(name="banks", bufs=5))
         sums = ctx.enter_context(tc.psum_pool(name="sums", bufs=GATES))
@@ -67,26 +69,20 @@ def tile_treelstm_pb_s_kernel(
         nc.vector.memset(bias_rows[:], 0.0)
         ident = keep.tile([P, P], F32, name="ident")
         make_identity(nc, ident[:])
-        idle_rows = keep.tile([P, SIZE], BF16, align_bytes=64, name="idle_rows")
-        idle_codes = keep.tile([P, WORDS], U32, align_bytes=64, name="idle_codes")
-        idle_scales = keep.tile([P, WORDS], U8, align_bytes=64, name="idle_scales")
-        nc.vector.memset(idle_rows[:], 0.0)
-        nc.vector.quantize_mx(
-            out=idle_codes[:].bitcast(FP8X4), scales=idle_scales[:], in_=idle_rows[:]
-        )
         warm = keep.tile([P, 1], F32, name="warm")
         nc.vector.memset(warm[:], 0.0)
         nc.scalar.activation(out=warm[:], in_=warm[:], func=ACT.Sigmoid)
 
+        h_rows = keep.tile([P, CH], BF16, name="h_rows")
+        nc.sync.dma_start(out=h_rows[:], in_=h_tilde[:, :])
+        z_rows = keep.tile([P, SIZE], BF16, name="z_rows")
+        nc.sync.dma_start(out=z_rows[:], in_=z0[:, :])
         for g in range(GATES):
             nc.sync.dma_start(
                 out=bias_rows[g : g + 1, :], in_=b_dram[g].rearrange("(o c) -> o c", o=1)
             )
-        z_rows = keep.tile([P, SIZE], BF16, name="z_rows")
-        nc.sync.dma_start(out=z_rows[:], in_=z0[:, :])
-        h_rows = keep.tile([P, CH], BF16, name="h_rows")
-        nc.sync.dma_start(out=h_rows[:], in_=h_tilde[:, :])
         u_rows = []
+        w_rows = []
         for g in range(GATES):
             rows = keep.tile([P, ROW_BLOCKS * CH], BF16, name="u_rows_%d" % g)
             nc.sync.dma_start(
@@ -94,89 +90,75 @@ def tile_treelstm_pb_s_kernel(
                 in_=u_dram[g].rearrange("(b p) k -> p b k", p=P),
             )
             u_rows.append(rows)
-        w_rows = []
-        for g in range(GATES):
-            for b in range(ROW_BLOCKS):
-                rows = w_pool.tile([P, SIZE], BF16, name="w_rows")
-                nc.sync.dma_start(out=rows[:], in_=w_dram[g][b * P : (b + 1) * P, :])
-                w_rows.append(rows)
+            rows = keep.tile([P, ROW_BLOCKS * SIZE], BF16, name="w_rows_%d" % g)
+            if g < GATES - 1:
+                nc.sync.dma_start(
+                    out=rows[:].rearrange("p (b k) -> p b k", b=ROW_BLOCKS),
+                    in_=w_dram[g].rearrange("(b p) k -> p b k", p=P),
+                )
+            else:
+                for b in range(ROW_BLOCKS):
+                    nc.sync.dma_start(
+                        out=rows[:, b * SIZE : (b + 1) * SIZE],
+                        in_=w_dram[g][b * P : (b + 1) * P, :],
+                    )
+            w_rows.append(rows)
         fc = keep.tile([P, CH], BF16, name="fc")
         nc.sync.dma_start(out=fc[:], in_=fc_sum[:, :])
 
-        bank = banks.tile([P, BANK_SLOTS, P], F32, tag="bank", name="bank")
-        for n in range(WARM_UP):
-            nc.tensor.matmul_mx(
-                out=bank[:].rearrange("p s r -> p (s r)")[:, 0:WORDS],
-                lhsT=idle_codes[:, 0:P].bitcast(FP8X4),
-                lhsT_scale=idle_scales[:, 0:P],
-                rhs=idle_codes[:].bitcast(FP8X4),
-                rhs_scale=idle_scales[:],
-                start=True,
-                stop=True,
-            )
+        bank = transpose_words(nc, banks, word_blocks(h_rows[:]), ident)
+        h_pairs = keep.tile([P, P], F32, name="h_pairs")
+        nc.vector.tensor_copy(out=h_pairs[:], in_=bank[:, 0, :])
 
-        bank = banks.tile([P, BANK_SLOTS, P], F32, tag="bank", name="bank")
-        transpose_pairs(nc, bank, 0, bias_rows[:].bitcast(F32), ident)
+        z_codes = keep.tile([P, WORDS], U32, align_bytes=64, name="z_codes")
+        z_scales = keep.tile([P, WORDS], U8, align_bytes=64, name="z_scales")
+        z_bank = transpose_words(nc, banks, word_blocks(z_rows[:]), ident)
+        bank = transpose_words(nc, banks, word_blocks(bias_rows[:]), ident)
         bias_cols = keep.tile([P, GATES], F32, name="bias_cols")
         nc.vector.tensor_copy(out=bias_cols[:], in_=bank[:, 0, 0:GATES])
-
-        z_bank = transpose_rows(nc, banks, z_rows, ident)
-
-        bank = banks.tile([P, BANK_SLOTS, P], F32, tag="bank", name="bank")
-        for g in range(GATES):
-            transpose_pairs(nc, bank, g, bias_cols[:, g : g + 1].to_broadcast([P, P]), ident)
+        pack_rows(nc, stage, z_bank, z_codes[:], z_scales[:])
+        bank = transpose_words(
+            nc, banks, [bias_cols[:, g : g + 1].to_broadcast([P, P]) for g in range(GATES)], ident
+        )
         bias_all = keep.tile([P, GATES * CH], BF16, name="bias_all")
         nc.vector.tensor_copy(
             out=bias_all[:].bitcast(F32).rearrange("p (g w) -> p g w", g=GATES),
             in_=bank[:, 0:GATES, :],
         )
 
-        z_codes = keep.tile([P, WORDS], U32, align_bytes=64, name="z_codes")
-        z_scales = keep.tile([P, WORDS], U8, align_bytes=64, name="z_scales")
-        pack_rows(nc, stage, z_bank, z_codes[:], z_scales[:])
-
-        blocks = [u_rows[g][:].bitcast(F32)[:, b * P : (b + 1) * P]
-                  for g in range(GATES) for b in range(ROW_BLOCKS)]
-        blocks.append(h_rows[:].bitcast(F32))
-        pairs_t = keep.tile([P, len(blocks), P], F32, name="pairs_t")
-        for first in range(0, len(blocks), BANK_SLOTS):
-            group = blocks[first : first + BANK_SLOTS]
-            bank = banks.tile([P, BANK_SLOTS, P], F32, tag="bank", name="bank")
-            for slot in range(len(group)):
-                transpose_pairs(nc, bank, slot, group[slot], ident)
-            nc.vector.tensor_copy(
-                out=pairs_t[:, first : first + len(group), :], in_=bank[:, 0 : len(group), :]
-            )
-        by_parity = pairs_t[:].rearrange("p s r -> p (s r)").bitcast(BF16).rearrange(
-            "p (c e) -> p c e", e=2
-        )
-        h_first = GATES * CH
-
-        w_codes = keep.tile([P, len(w_rows), WORDS], U32, align_bytes=64, name="w_codes")
-        w_scales = keep.tile([P, len(w_rows), WORDS], U8, align_bytes=64, name="w_scales")
+        w_codes = keep.tile([P, GATES * ROW_BLOCKS, WORDS], U32, align_bytes=64, name="w_codes")
+        w_scales = keep.tile([P, GATES * ROW_BLOCKS, WORDS], U8, align_bytes=64, name="w_scales")
         plain = []
         for g in range(GATES):
+            bank = transpose_words(nc, banks, word_blocks(u_rows[g][:]), ident)
+            u_pairs = keep.tile([P, CH], F32, name="u_pairs_%d" % g)
+            nc.scalar.copy(
+                out=u_pairs[:].rearrange("p (b r) -> p b r", b=ROW_BLOCKS),
+                in_=bank[:, 0:ROW_BLOCKS, :],
+            )
+            w_blocks = word_blocks(w_rows[g][:])
+            per_block = len(w_blocks) // ROW_BLOCKS
+            w_banks = [
+                transpose_words(nc, banks, w_blocks[b * per_block : (b + 1) * per_block], ident)
+                for b in range(ROW_BLOCKS)
+            ]
             plain_ps = sums.tile([P, CH], F32, tag="sums", name="plain_ps")
-            for e in range(ROW_BLOCKS):
-                j = g * ROW_BLOCKS + e
-                w_bank = transpose_rows(nc, banks, w_rows[j], ident)
+            for e in range(2):
                 nc.tensor.matmul(
                     out=plain_ps[:],
-                    lhsT=by_parity[:, h_first : h_first + P, e],
-                    rhs=by_parity[:, g * CH : (g + 1) * CH, e],
+                    lhsT=by_parity(h_pairs, e),
+                    rhs=by_parity(u_pairs, e),
                     start=(e == 0),
                     stop=(e == 1),
                 )
-                if e == 1:
-                    plain_sb = keep.tile([P, CH], F32, name="plain_%d" % g)
-                    nc.vector.tensor_tensor(
-                        out=plain_sb[:],
-                        in0=plain_ps[:],
-                        in1=bias_all[:, g * CH : (g + 1) * CH],
-                        op=ALU.add,
-                    )
-                    plain.append(plain_sb)
-                pack_rows(nc, stage, w_bank, w_codes[:, j, :], w_scales[:, j, :])
+            j = g * ROW_BLOCKS
+            pack_rows(nc, stage, w_banks[0], w_codes[:, j, :], w_scales[:, j, :])
+            plain_sb = keep.tile([P, CH], F32, name="plain_%d" % g)
+            nc.vector.tensor_tensor(
+                out=plain_sb[:], in0=plain_ps[:], in1=bias_all[:, g * CH : (g + 1) * CH], op=ALU.add
+            )
+            plain.append(plain_sb)
+            pack_rows(nc, stage, w_banks[1], w_codes[:, j + 1, :], w_scales[:, j + 1, :])
 
         acts = []
         for g in range(GATES):

@@ -49,6 +49,14 @@ def by_parity(pairs, e):
     return pairs[:].bitcast(BF16).rearrange("p (c e) -> p c e", e=2)[:, :, e]
 
 
+def from_blocks(sums_ps):
+    return sums_ps.rearrange("p (b r) -> p r b", b=ROW_BLOCKS)
+
+
+def channels(ap):
+    return ap.rearrange("p (r b) -> p r b", b=ROW_BLOCKS)
+
+
 def tile_treelstm_pb_s_kernel(
     tc, z0, h_tilde, fc_sum, W_i, U_i, b_i, W_o, U_o, b_o, W_u, U_u, b_u, out
 ):
@@ -86,21 +94,19 @@ def tile_treelstm_pb_s_kernel(
         for g in range(GATES):
             rows = keep.tile([P, ROW_BLOCKS * CH], BF16, name="u_rows_%d" % g)
             nc.sync.dma_start(
-                out=rows[:].rearrange("p (b k) -> p b k", b=ROW_BLOCKS),
-                in_=u_dram[g].rearrange("(b p) k -> p b k", p=P),
+                out=rows[:], in_=u_dram[g].rearrange("(p b) k -> p (b k)", b=ROW_BLOCKS)
             )
             u_rows.append(rows)
             rows = keep.tile([P, ROW_BLOCKS * SIZE], BF16, name="w_rows_%d" % g)
             if g < GATES - 1:
                 nc.sync.dma_start(
-                    out=rows[:].rearrange("p (b k) -> p b k", b=ROW_BLOCKS),
-                    in_=w_dram[g].rearrange("(b p) k -> p b k", p=P),
+                    out=rows[:], in_=w_dram[g].rearrange("(p b) k -> p (b k)", b=ROW_BLOCKS)
                 )
             else:
                 for b in range(ROW_BLOCKS):
                     nc.sync.dma_start(
                         out=rows[:, b * SIZE : (b + 1) * SIZE],
-                        in_=w_dram[g][b * P : (b + 1) * P, :],
+                        in_=w_dram[g].rearrange("(p b) k -> p b k", b=ROW_BLOCKS)[:, b, :],
                     )
             w_rows.append(rows)
         fc = keep.tile([P, CH], BF16, name="fc")
@@ -128,37 +134,44 @@ def tile_treelstm_pb_s_kernel(
 
         w_codes = keep.tile([P, GATES * ROW_BLOCKS, WORDS], U32, align_bytes=64, name="w_codes")
         w_scales = keep.tile([P, GATES * ROW_BLOCKS, WORDS], U8, align_bytes=64, name="w_scales")
-        plain = []
-        for g in range(GATES):
+        def transposed_u(g):
             bank = transpose_words(nc, banks, word_blocks(u_rows[g][:]), ident)
-            u_pairs = keep.tile([P, CH], F32, name="u_pairs_%d" % g)
-            nc.scalar.copy(
-                out=u_pairs[:].rearrange("p (b r) -> p b r", b=ROW_BLOCKS),
+            pairs = keep.tile([P, CH], F32, name="u_pairs_%d" % g)
+            nc.vector.tensor_copy(
+                out=pairs[:].rearrange("p (b r) -> p b r", b=ROW_BLOCKS),
                 in_=bank[:, 0:ROW_BLOCKS, :],
             )
+            return pairs
+
+        plain = []
+        u_pairs = [transposed_u(0)]
+        for g in range(GATES):
             w_blocks = word_blocks(w_rows[g][:])
             per_block = len(w_blocks) // ROW_BLOCKS
-            w_banks = [
-                transpose_words(nc, banks, w_blocks[b * per_block : (b + 1) * per_block], ident)
-                for b in range(ROW_BLOCKS)
-            ]
+            j = g * ROW_BLOCKS
+            w_bank = transpose_words(nc, banks, w_blocks[0:per_block], ident)
+            if g + 1 < GATES:
+                u_pairs.append(transposed_u(g + 1))
+            pack_rows(nc, stage, w_bank, w_codes[:, j, :], w_scales[:, j, :])
+            w_bank = transpose_words(nc, banks, w_blocks[per_block : 2 * per_block], ident)
             plain_ps = sums.tile([P, CH], F32, tag="sums", name="plain_ps")
             for e in range(2):
                 nc.tensor.matmul(
                     out=plain_ps[:],
                     lhsT=by_parity(h_pairs, e),
-                    rhs=by_parity(u_pairs, e),
+                    rhs=by_parity(u_pairs[g], e),
                     start=(e == 0),
                     stop=(e == 1),
                 )
-            j = g * ROW_BLOCKS
-            pack_rows(nc, stage, w_banks[0], w_codes[:, j, :], w_scales[:, j, :])
             plain_sb = keep.tile([P, CH], F32, name="plain_%d" % g)
             nc.vector.tensor_tensor(
-                out=plain_sb[:], in0=plain_ps[:], in1=bias_all[:, g * CH : (g + 1) * CH], op=ALU.add
+                out=channels(plain_sb[:]),
+                in0=from_blocks(plain_ps[:]),
+                in1=channels(bias_all[:, g * CH : (g + 1) * CH]),
+                op=ALU.add,
             )
             plain.append(plain_sb)
-            pack_rows(nc, stage, w_banks[1], w_codes[:, j + 1, :], w_scales[:, j + 1, :])
+            pack_rows(nc, stage, w_bank, w_codes[:, j + 1, :], w_scales[:, j + 1, :])
 
         acts = []
         for g in range(GATES):
@@ -177,7 +190,9 @@ def tile_treelstm_pb_s_kernel(
                         stop=(k_pass == PASSES - 1),
                     )
             pre = keep.tile([P, CH], F32, name="pre_%d" % g)
-            nc.vector.tensor_tensor(out=pre[:], in0=mx_ps[:], in1=plain[g][:], op=ALU.add)
+            nc.vector.tensor_tensor(
+                out=channels(pre[:]), in0=from_blocks(mx_ps[:]), in1=channels(plain[g][:]), op=ALU.add
+            )
             act = keep.tile([P, CH], F32, name="act_%d" % g)
             nc.scalar.activation(out=act[:], in_=pre[:], func=gate_func[g])
             acts.append(act)

@@ -20,6 +20,8 @@ PASSES = SIZE // (4 * P)
 HALVES = 2
 WORDS = PASSES * P
 BANK_SLOTS = 4
+WARM_UP = 14
+IDLE_RUN = 4
 
 FLOPS = 2 * P * GATES * CH * (SIZE + CH)
 
@@ -69,14 +71,36 @@ def tile_treelstm_pb_s_kernel(
     with ExitStack() as ctx:
         keep = ctx.enter_context(tc.tile_pool(name="keep", bufs=1))
         stage = ctx.enter_context(tc.tile_pool(name="stage", bufs=4))
-        banks = ctx.enter_context(tc.psum_pool(name="banks", bufs=5))
+        banks = ctx.enter_context(tc.psum_pool(name="banks", bufs=4))
         sums = ctx.enter_context(tc.psum_pool(name="sums", bufs=GATES))
+        idle_pool = ctx.enter_context(tc.psum_pool(name="idle", bufs=1))
         ctx.enter_context(tc.manual_schedule())
 
         bias_rows = keep.tile([P, CH], BF16, name="bias_rows")
         nc.vector.memset(bias_rows[:], 0.0)
         ident = keep.tile([P, P], F32, name="ident")
         make_identity(nc, ident[:])
+        idle_rows = keep.tile([P, 4 * P], BF16, align_bytes=64, name="idle_rows")
+        idle_codes = keep.tile([P, P], U32, align_bytes=64, name="idle_codes")
+        idle_scales = keep.tile([P, P], U8, align_bytes=64, name="idle_scales")
+        idle_ps = idle_pool.tile([P, P], F32, name="idle_ps")
+        nc.vector.memset(idle_rows[:].bitcast(F32), 0.0)
+        nc.vector.quantize_mx(
+            out=idle_codes[:].bitcast(FP8X4), scales=idle_scales[:], in_=idle_rows[:]
+        )
+
+        def idle_passes(count):
+            for n in range(count):
+                nc.tensor.matmul_mx(
+                    out=idle_ps[:],
+                    lhsT=idle_codes[:].bitcast(FP8X4),
+                    lhsT_scale=idle_scales[:],
+                    rhs=idle_codes[:].bitcast(FP8X4),
+                    rhs_scale=idle_scales[:],
+                    start=True,
+                    stop=True,
+                )
+
         warm = keep.tile([P, 1], F32, name="warm")
         nc.vector.memset(warm[:], 0.0)
         nc.scalar.activation(out=warm[:], in_=warm[:], func=ACT.Sigmoid)
@@ -112,6 +136,8 @@ def tile_treelstm_pb_s_kernel(
         fc = keep.tile([P, CH], BF16, name="fc")
         nc.sync.dma_start(out=fc[:], in_=fc_sum[:, :])
 
+        idle_passes(WARM_UP)
+
         bank = transpose_words(nc, banks, word_blocks(h_rows[:]), ident)
         h_pairs = keep.tile([P, P], F32, name="h_pairs")
         nc.vector.tensor_copy(out=h_pairs[:], in_=bank[:, 0, :])
@@ -122,6 +148,7 @@ def tile_treelstm_pb_s_kernel(
         bank = transpose_words(nc, banks, word_blocks(bias_rows[:]), ident)
         bias_cols = keep.tile([P, GATES], F32, name="bias_cols")
         nc.vector.tensor_copy(out=bias_cols[:], in_=bank[:, 0, 0:GATES])
+        idle_passes(IDLE_RUN)
         pack_rows(nc, stage, z_bank, z_codes[:], z_scales[:])
         bank = transpose_words(
             nc, banks, [bias_cols[:, g : g + 1].to_broadcast([P, P]) for g in range(GATES)], ident
@@ -145,6 +172,7 @@ def tile_treelstm_pb_s_kernel(
 
         plain = []
         u_pairs = [transposed_u(0)]
+        idle_passes(IDLE_RUN)
         for g in range(GATES):
             w_blocks = word_blocks(w_rows[g][:])
             per_block = len(w_blocks) // ROW_BLOCKS

from contextlib import ExitStack

import concourse.mybir as mybir
from concourse.masks import make_identity

F32 = mybir.dt.float32
BF16 = mybir.dt.bfloat16
U32 = mybir.dt.uint32
U8 = mybir.dt.uint8
FP8X4 = mybir.dt.float8_e4m3fn_x4
ACT = mybir.ActivationFunctionType
ALU = mybir.AluOpType

P = 128
SIZE = 1024
CH = 256
GATES = 3
ROW_BLOCKS = CH // P
PASSES = SIZE // (4 * P)
HALVES = 2
WORDS = PASSES * P
BANK_SLOTS = 4
WARM_UP = 14
IDLE_RUN = 4

FLOPS = 2 * P * GATES * CH * (SIZE + CH)


def word_blocks(rows):
    words = rows.bitcast(F32)
    return [words[:, s * P : (s + 1) * P] for s in range(words.shape[1] // P)]


def transpose_words(nc, banks, blocks, ident):
    bank = banks.tile([P, BANK_SLOTS, P], F32, tag="bank", name="bank")
    for slot in range(len(blocks)):
        nc.tensor.transpose(out=bank[:, slot, :], in_=blocks[slot], identity=ident[:])
    return bank


def pack_rows(nc, stage, bank, codes, scales):
    grouped = stage.tile([P, SIZE], BF16, align_bytes=64, name="grouped")
    nc.scalar.copy(
        out=grouped[:].bitcast(F32).rearrange("p (g r u) -> p g r u", g=PASSES, u=HALVES),
        in_=bank[:].rearrange("p (g u) r -> p g r u", u=HALVES),
    )
    nc.vector.quantize_mx(out=codes.bitcast(FP8X4), scales=scales, in_=grouped[:])


def by_parity(pairs, e):
    return pairs[:].bitcast(BF16).rearrange("p (c e) -> p c e", e=2)[:, :, e]


def from_blocks(sums_ps):
    return sums_ps.rearrange("p (b r) -> p r b", b=ROW_BLOCKS)


def channels(ap):
    return ap.rearrange("p (r b) -> p r b", b=ROW_BLOCKS)


def tile_treelstm_pb_s_kernel(
    tc, z0, h_tilde, fc_sum, W_i, U_i, b_i, W_o, U_o, b_o, W_u, U_u, b_u, out
):
    nc = tc.nc
    w_dram = (W_i, W_u, W_o)
    u_dram = (U_i, U_u, U_o)
    b_dram = (b_i, b_u, b_o)
    gate_func = (ACT.Sigmoid, ACT.Tanh, ACT.Sigmoid)

    with ExitStack() as ctx:
        keep = ctx.enter_context(tc.tile_pool(name="keep", bufs=1))
        stage = ctx.enter_context(tc.tile_pool(name="stage", bufs=4))
        banks = ctx.enter_context(tc.psum_pool(name="banks", bufs=4))
        sums = ctx.enter_context(tc.psum_pool(name="sums", bufs=GATES))
        idle_pool = ctx.enter_context(tc.psum_pool(name="idle", bufs=1))
        ctx.enter_context(tc.manual_schedule())

        bias_rows = keep.tile([P, CH], BF16, name="bias_rows")
        nc.vector.memset(bias_rows[:], 0.0)
        ident = keep.tile([P, P], F32, name="ident")
        make_identity(nc, ident[:])
        idle_rows = keep.tile([P, 4 * P], BF16, align_bytes=64, name="idle_rows")
        idle_codes = keep.tile([P, P], U32, align_bytes=64, name="idle_codes")
        idle_scales = keep.tile([P, P], U8, align_bytes=64, name="idle_scales")
        idle_ps = idle_pool.tile([P, P], F32, name="idle_ps")
        nc.vector.memset(idle_rows[:].bitcast(F32), 0.0)
        nc.vector.quantize_mx(
            out=idle_codes[:].bitcast(FP8X4), scales=idle_scales[:], in_=idle_rows[:]
        )

        def idle_passes(count):
            for n in range(count):
                nc.tensor.matmul_mx(
                    out=idle_ps[:],
                    lhsT=idle_codes[:].bitcast(FP8X4),
                    lhsT_scale=idle_scales[:],
                    rhs=idle_codes[:].bitcast(FP8X4),
                    rhs_scale=idle_scales[:],
                    start=True,
                    stop=True,
                )

        warm = keep.tile([P, 1], F32, name="warm")
        nc.vector.memset(warm[:], 0.0)
        nc.scalar.activation(out=warm[:], in_=warm[:], func=ACT.Sigmoid)

        h_rows = keep.tile([P, CH], BF16, name="h_rows")
        nc.sync.dma_start(out=h_rows[:], in_=h_tilde[:, :])
        z_rows = keep.tile([P, SIZE], BF16, name="z_rows")
        nc.sync.dma_start(out=z_rows[:], in_=z0[:, :])
        for g in range(GATES):
            nc.sync.dma_start(
                out=bias_rows[g : g + 1, :], in_=b_dram[g].rearrange("(o c) -> o c", o=1)
            )
        u_rows = []
        w_rows = []
        for g in range(GATES):
            rows = keep.tile([P, ROW_BLOCKS * CH], BF16, name="u_rows_%d" % g)
            nc.sync.dma_start(
                out=rows[:], in_=u_dram[g].rearrange("(p b) k -> p (b k)", b=ROW_BLOCKS)
            )
            u_rows.append(rows)
            rows = keep.tile([P, ROW_BLOCKS * SIZE], BF16, name="w_rows_%d" % g)
            if g < GATES - 1:
                nc.sync.dma_start(
                    out=rows[:], in_=w_dram[g].rearrange("(p b) k -> p (b k)", b=ROW_BLOCKS)
                )
            else:
                for b in range(ROW_BLOCKS):
                    nc.sync.dma_start(
                        out=rows[:, b * SIZE : (b + 1) * SIZE],
                        in_=w_dram[g].rearrange("(p b) k -> p b k", b=ROW_BLOCKS)[:, b, :],
                    )
            w_rows.append(rows)
        fc = keep.tile([P, CH], BF16, name="fc")
        nc.sync.dma_start(out=fc[:], in_=fc_sum[:, :])

        idle_passes(WARM_UP)

        bank = transpose_words(nc, banks, word_blocks(h_rows[:]), ident)
        h_pairs = keep.tile([P, P], F32, name="h_pairs")
        nc.vector.tensor_copy(out=h_pairs[:], in_=bank[:, 0, :])

        z_codes = keep.tile([P, WORDS], U32, align_bytes=64, name="z_codes")
        z_scales = keep.tile([P, WORDS], U8, align_bytes=64, name="z_scales")
        z_bank = transpose_words(nc, banks, word_blocks(z_rows[:]), ident)
        bank = transpose_words(nc, banks, word_blocks(bias_rows[:]), ident)
        bias_cols = keep.tile([P, GATES], F32, name="bias_cols")
        nc.vector.tensor_copy(out=bias_cols[:], in_=bank[:, 0, 0:GATES])
        idle_passes(IDLE_RUN)
        pack_rows(nc, stage, z_bank, z_codes[:], z_scales[:])
        bank = transpose_words(
            nc, banks, [bias_cols[:, g : g + 1].to_broadcast([P, P]) for g in range(GATES)], ident
        )
        bias_all = keep.tile([P, GATES * CH], BF16, name="bias_all")
        nc.vector.tensor_copy(
            out=bias_all[:].bitcast(F32).rearrange("p (g w) -> p g w", g=GATES),
            in_=bank[:, 0:GATES, :],
        )

        w_codes = keep.tile([P, GATES * ROW_BLOCKS, WORDS], U32, align_bytes=64, name="w_codes")
        w_scales = keep.tile([P, GATES * ROW_BLOCKS, WORDS], U8, align_bytes=64, name="w_scales")
        def transposed_u(g):
            bank = transpose_words(nc, banks, word_blocks(u_rows[g][:]), ident)
            pairs = keep.tile([P, CH], F32, name="u_pairs_%d" % g)
            nc.vector.tensor_copy(
                out=pairs[:].rearrange("p (b r) -> p b r", b=ROW_BLOCKS),
                in_=bank[:, 0:ROW_BLOCKS, :],
            )
            return pairs

        plain = []
        u_pairs = [transposed_u(0)]
        idle_passes(IDLE_RUN)
        for g in range(GATES):
            w_blocks = word_blocks(w_rows[g][:])
            per_block = len(w_blocks) // ROW_BLOCKS
            j = g * ROW_BLOCKS
            w_bank = transpose_words(nc, banks, w_blocks[0:per_block], ident)
            if g + 1 < GATES:
                u_pairs.append(transposed_u(g + 1))
            pack_rows(nc, stage, w_bank, w_codes[:, j, :], w_scales[:, j, :])
            w_bank = transpose_words(nc, banks, w_blocks[per_block : 2 * per_block], ident)
            plain_ps = sums.tile([P, CH], F32, tag="sums", name="plain_ps")
            for e in range(2):
                nc.tensor.matmul(
                    out=plain_ps[:],
                    lhsT=by_parity(h_pairs, e),
                    rhs=by_parity(u_pairs[g], e),
                    start=(e == 0),
                    stop=(e == 1),
                )
            plain_sb = keep.tile([P, CH], F32, name="plain_%d" % g)
            nc.vector.tensor_tensor(
                out=channels(plain_sb[:]),
                in0=from_blocks(plain_ps[:]),
                in1=channels(bias_all[:, g * CH : (g + 1) * CH]),
                op=ALU.add,
            )
            plain.append(plain_sb)
            pack_rows(nc, stage, w_bank, w_codes[:, j + 1, :], w_scales[:, j + 1, :])

        acts = []
        for g in range(GATES):
            mx_ps = sums.tile([P, CH], F32, tag="sums", name="mx_ps")
            for b in range(ROW_BLOCKS):
                j = g * ROW_BLOCKS + b
                for k_pass in range(PASSES):
                    cols = slice(k_pass * P, (k_pass + 1) * P)
                    nc.tensor.matmul_mx(
                        out=mx_ps[:, b * P : (b + 1) * P],
                        lhsT=z_codes[:, cols].bitcast(FP8X4),
                        lhsT_scale=z_scales[:, cols],
                        rhs=w_codes[:, j, cols].bitcast(FP8X4),
                        rhs_scale=w_scales[:, j, cols],
                        start=(k_pass == 0),
                        stop=(k_pass == PASSES - 1),
                    )
            pre = keep.tile([P, CH], F32, name="pre_%d" % g)
            nc.vector.tensor_tensor(
                out=channels(pre[:]), in0=from_blocks(mx_ps[:]), in1=channels(plain[g][:]), op=ALU.add
            )
            act = keep.tile([P, CH], F32, name="act_%d" % g)
            nc.scalar.activation(out=act[:], in_=pre[:], func=gate_func[g])
            acts.append(act)
        act_i, act_u, act_o = acts

        c_sb = keep.tile([P, CH], F32, name="c_sb")
        nc.vector.tensor_tensor(out=c_sb[:], in0=act_i[:], in1=act_u[:], op=ALU.mult)
        nc.vector.tensor_tensor(out=c_sb[:], in0=c_sb[:], in1=fc[:], op=ALU.add)
        nc.sync.dma_start(out=out[:, CH : 2 * CH], in_=c_sb[:])
        tanh_c = keep.tile([P, CH], F32, name="tanh_c")
        nc.scalar.activation(out=tanh_c[:], in_=c_sb[:], func=ACT.Tanh)
        h_sb = keep.tile([P, CH], F32, name="h_sb")
        nc.vector.tensor_tensor(out=h_sb[:], in0=act_o[:], in1=tanh_c[:], op=ALU.mult)
        nc.sync.dma_start(out=out[:, 0:CH], in_=h_sb[:])
